import numpy as np
import ml_dtypes


BF16 = ml_dtypes.bfloat16


def bf(x):
    return np.asarray(x, np.float32).astype(BF16)


def f64(x):
    return np.asarray(x).astype(np.float64)


E2M1 = np.array([0.0, 0.5, 1.0, 1.5, 2.0, 3.0, 4.0, 6.0, -0.0, -0.5, -1.0, -1.5, -2.0, -3.0, -4.0, -6.0])


def pack_weight(w, fmt):
    k, n = w.shape
    w = f64(bf(w)).reshape(k // 32, 32, n)
    amax = np.abs(w).max(1)
    if fmt == "e4m3":
        byte = np.frexp(amax)[1] - 1 + 127 - 7
    else:
        mant, ex = np.frexp(amax / 6.0)
        byte = np.where(mant > 0.5, ex, ex - 1) + 127
    byte = np.clip(np.where(amax > 0, byte, 1), 1, 254)
    scaled = (w * np.exp2(127.0 - byte)[:, None, :]).reshape(k, n).astype(np.float32)
    by_word = np.ascontiguousarray(scaled.reshape(k // 512, 128, 4, n).transpose(0, 1, 3, 2))
    if fmt == "e4m3":
        words = by_word.astype(ml_dtypes.float8_e4m3fn).view(np.uint8)
    else:
        c = by_word.astype(ml_dtypes.float4_e2m1fn).view(np.uint8) & 0xF
        words = c[..., 0::2] | (c[..., 1::2] << 4)
    return np.ascontiguousarray(words), np.ascontiguousarray(byte.astype(np.uint8).reshape(k // 512, 16, n))


def unpack_weight(words, scales, fmt):
    g, p, n, _ = words.shape
    if fmt == "e4m3":
        vals = np.ascontiguousarray(words).view(ml_dtypes.float8_e4m3fn).astype(np.float64)
    else:
        nib = np.empty((g, p, n, 4), np.uint8)
        nib[..., 0::2] = words & 0xF
        nib[..., 1::2] = words >> 4
        vals = E2M1[nib]
    vals = vals * np.repeat(np.exp2(scales.astype(np.float64) - 127.0), 8, axis=1)[..., None]
    return vals.transpose(0, 1, 3, 2).reshape(g * 512, n)

def pack4(w):
    words, scales = pack_weight(w, "e2m1")
    return words.reshape(words.shape[0], 128, -1), scales


def unpack4(words, scales):
    return unpack_weight(words.reshape(words.shape[0], 128, -1, 2), scales, "e2m1")


def kspread(k):
    return np.exp2(np.repeat(np.random.randint(-6, 7, k // 32), 32).astype(np.float64))


B, N, C, H = 2, 64, 3072, 16
EPS = 1e-6


def rmsnorm(v, w):
    var = np.mean(np.square(v), axis=-1, keepdims=True)
    return v * (1.0 / np.sqrt(var + EPS)) * w


def setup_inputs():
    s = kspread(C)
    x = np.random.standard_normal((B, N, C)) * s
    x_words, x_scales = pack4(np.ascontiguousarray(x.reshape(B * N, C).T))
    w = np.random.standard_normal((3 * C, C)) / np.sqrt(C) / s[None, :]
    words, scales = pack4(np.ascontiguousarray(w.T))
    q_norm_w = bf(1.0 + 0.1 * np.random.standard_normal(C))
    k_norm_w = bf(1.0 + 0.1 * np.random.standard_normal(C))
    return {"x_words": x_words,
            "x_scales": x_scales,
            "w_qkv_words": words,
            "w_qkv_scales": scales,
            "q_norm_w": q_norm_w,
            "k_norm_w": k_norm_w}


def reference(x_words, x_scales, w_qkv_words, w_qkv_scales, q_norm_w, k_norm_w):
    xq = unpack4(x_words, x_scales).T.reshape(B, N, C)
    wt = unpack4(w_qkv_words, w_qkv_scales)
    q = xq @ wt[:, :C]
    k = xq @ wt[:, C:2 * C]
    v = xq @ wt[:, 2 * C:]
    return rmsnorm(q, f64(q_norm_w)), rmsnorm(k, f64(k_norm_w)), v

@@ -1,0 +1,166 @@
+from contextlib import ExitStack
+
+import concourse.mybir as mybir
+
+F32 = mybir.dt.float32
+BF16 = mybir.dt.bfloat16
+I32 = mybir.dt.int32
+U8 = mybir.dt.uint8
+FP4X4 = mybir.dt.float4_e2m1fn_x4
+ACT = mybir.ActivationFunctionType
+ALU = mybir.AluOpType
+
+P = 128
+HID = 3072
+PASSES = HID // 512
+THIRDS = 3
+NT = 512
+TILES = HID // NT
+RUN = 3
+CHUNKS = THIRDS * PASSES
+EPS = 1e-6
+
+FLOPS = 2 * P * HID * THIRDS * HID
+
+
+def tile_internattention_pa_kernel(
+    tc, x_words, x_scales, w_qkv_words, w_qkv_scales, q_norm_w, k_norm_w, out_0, out_1, out_2
+):
+    nc = tc.nc
+    outs = [out_0.flatten_outer_dims(), out_1.flatten_outer_dims(), out_2.flatten_outer_dims()]
+
+    with ExitStack() as ctx:
+        ctx.enter_context(tc.manual_schedule())
+        keep = ctx.enter_context(tc.tile_pool(name="keep", bufs=1))
+        scrap = ctx.enter_context(tc.tile_pool(name="scrap", bufs=2))
+        acc_pool = ctx.enter_context(tc.psum_pool(name="acc_pool", bufs=TILES))
+        aux_pool = ctx.enter_context(tc.psum_pool(name="aux_pool", bufs=2))
+
+        x_codes = keep.tile([P, PASSES, 256], U8, name="x_codes", align_bytes=64)
+        x_plane = keep.tile([P, PASSES, P], U8, name="x_plane", align_bytes=64)
+        w_codes = [
+            keep.tile([P, 2 * HID], U8, name="w_codes%d" % c, align_bytes=64) for c in range(CHUNKS)
+        ]
+        w_plane = [
+            keep.tile([P, RUN, HID], U8, name="w_plane%d" % r, align_bytes=64)
+            for r in range(CHUNKS // RUN)
+        ]
+        warm = keep.tile([P, 2], F32, name="warm")
+        ones = keep.tile([P, P], BF16, name="ones")
+        gain_row = keep.tile([P, 2 * HID], BF16, name="gain_row")
+        gain = keep.tile([P, 2 * HID], BF16, name="gain")
+        result = [keep.tile([P, HID], F32, name="result%d" % t) for t in range(THIRDS)]
+        stats = [keep.tile([P, 16], F32, name="stats%d" % t) for t in range(2)]
+
+        def load_codes(c):
+            t, g = divmod(c, PASSES)
+            nc.sync.dma_start(
+                out=w_codes[c][:].bitcast(I32),
+                in_=w_qkv_words[g, :, 2 * HID * t : 2 * HID * (t + 1)].bitcast(I32),
+            )
+
+        def load_scale_rows(plane, rows):
+            for r in range(4):
+                nc.sync.dma_start(
+                    out=plane[r:P:32, :, :].bitcast(I32),
+                    in_=rows[:, r:16:4, :].rearrange("g q n -> q g n").bitcast(I32),
+                )
+
+        def load_run(r):
+            t, a = divmod(r, PASSES // RUN)
+            load_scale_rows(
+                w_plane[r], w_qkv_scales[RUN * a : RUN * (a + 1), :, HID * t : HID * (t + 1)]
+            )
+
+        nc.gpsimd.memset(warm[:, 0:1], 1.0)
+        nc.gpsimd.memset(ones[:], 1.0)
+        nc.scalar.activation(out=warm[:, 1:2], in_=warm[:, 0:1], func=ACT.Sqrt)
+
+        nc.sync.dma_start(
+            out=x_codes[:].bitcast(I32), in_=x_words.rearrange("g p b -> p g b").bitcast(I32)
+        )
+        load_codes(0)
+        nc.vector.memset(x_plane[:].bitcast(I32), 0)
+        nc.vector.memset(w_plane[0][:].bitcast(I32), 0)
+        nc.vector.memset(w_plane[1][:].bitcast(I32), 0)
+        nc.vector.memset(gain_row[:].bitcast(I32), 0)
+        for r in range(2, CHUNKS // RUN):
+            nc.vector.memset(w_plane[r][:].bitcast(I32), 0)
+        nc.scalar.dma_start(out=gain_row[0:1, 0:HID], in_=q_norm_w.rearrange("(o n) -> o n", o=1))
+        nc.scalar.dma_start(
+            out=gain_row[0:1, HID : 2 * HID], in_=k_norm_w.rearrange("(o n) -> o n", o=1)
+        )
+        load_scale_rows(x_plane, x_scales)
+        load_run(0)
+        for c in range(1, CHUNKS):
+            if (c + 1) % RUN == 0 and c + 1 < CHUNKS:
+                load_run((c + 1) // RUN)
+            load_codes(c)
+
+        def spread_gain(i):
+            cols = slice(NT * i, NT * (i + 1))
+            aux = aux_pool.tile([P, NT], F32, name="aux")
+            nc.tensor.matmul(out=aux[:], lhsT=ones[:], rhs=gain_row[:, cols], start=True, stop=True)
+            nc.scalar.copy(out=gain[:, cols], in_=aux[:])
+
+        for t in range(THIRDS):
+            acc = [acc_pool.tile([P, NT], F32, name="acc") for j in range(TILES)]
+            for g in range(PASSES):
+                c = PASSES * t + g
+                for j in range(TILES):
+                    nc.tensor.matmul_mx(
+                        out=acc[j][:],
+                        lhsT=x_codes[:, g, :].bitcast(FP4X4),
+                        lhsT_scale=x_plane[:, g, :],
+                        rhs=w_codes[c][:, 2 * NT * j : 2 * NT * (j + 1)].bitcast(FP4X4),
+                        rhs_scale=w_plane[c // RUN][:, c % RUN, NT * j : NT * (j + 1)],
+                        start=(g == 0),
+                        stop=(g == PASSES - 1),
+                    )
+                if t == 0:
+                    spread_gain(2 * g)
+                    spread_gain(2 * g + 1)
+            if t < 2:
+                for j in range(TILES):
+                    cols = slice(NT * j, NT * (j + 1))
+                    squares = scrap.tile([P, NT], BF16, name="squares")
+                    nc.scalar.activation(
+                        out=squares[:], in_=acc[j][:], func=ACT.Square, accum_out=stats[t][:, j : j + 1]
+                    )
+                    nc.vector.tensor_tensor(
+                        out=result[t][:, cols],
+                        in0=acc[j][:],
+                        in1=gain[:, HID * t + NT * j : HID * t + NT * (j + 1)],
+                        op=ALU.mult,
+                    )
+                nc.vector.tensor_scalar(
+                    out=stats[t][:, 8 : 8 + TILES],
+                    in0=stats[t][:, 0:TILES],
+                    scalar1=1.0 / HID,
+                    scalar2=EPS,
+                    op0=ALU.mult,
+                    op1=ALU.add,
+                    accum_out=stats[t][:, 14:15],
+                )
+                nc.scalar.activation(out=stats[t][:, 15:16], in_=stats[t][:, 14:15], func=ACT.Sqrt)
+                nc.vector.reciprocal(out=stats[t][:, 7:8], in_=stats[t][:, 15:16])
+                for h in range(2):
+                    cols = slice(HID // 2 * h, HID // 2 * (h + 1))
+                    nc.vector.tensor_scalar(
+                        out=result[t][:, cols],
+                        in0=result[t][:, cols],
+                        scalar1=stats[t][:, 7:8],
+                        scalar2=None,
+                        op0=ALU.mult,
+                    )
+                    queue = nc.scalar if t == 0 else nc.sync
+                    queue.dma_start(out=outs[t][:, cols], in_=result[t][:, cols])
+            else:
+                for j in range(TILES):
+                    cols = slice(NT * j, NT * (j + 1))
+                    if j % 2 == 0:
+                        nc.vector.tensor_copy(out=result[t][:, cols], in_=acc[j][:])
+                        nc.sync.dma_start(out=outs[t][:, cols], in_=result[t][:, cols])
+                    else:
+                        nc.scalar.copy(out=result[t][:, cols], in_=acc[j][:])
+                        nc.scalar.dma_start(out=outs[t][:, cols], in_=result[t][:, cols])

@@ -16,7 +16,7 @@ PASSES = HID // 512
 THIRDS = 3
 NT = 512
 TILES = HID // NT
-RUN = 3
+RUN = 2
 CHUNKS = THIRDS * PASSES
 EPS = 1e-6
 
@@ -81,20 +81,22 @@ def tile_internattention_pa_kernel(
         )
         load_codes(0)
         nc.vector.memset(x_plane[:].bitcast(I32), 0)
-        nc.vector.memset(w_plane[0][:].bitcast(I32), 0)
-        nc.vector.memset(w_plane[1][:].bitcast(I32), 0)
+        for r in range(3):
+            nc.vector.memset(w_plane[r][:].bitcast(I32), 0)
         nc.vector.memset(gain_row[:].bitcast(I32), 0)
-        for r in range(2, CHUNKS // RUN):
+        for r in range(3, CHUNKS // RUN):
             nc.vector.memset(w_plane[r][:].bitcast(I32), 0)
         nc.scalar.dma_start(out=gain_row[0:1, 0:HID], in_=q_norm_w.rearrange("(o n) -> o n", o=1))
         nc.scalar.dma_start(
             out=gain_row[0:1, HID : 2 * HID], in_=k_norm_w.rearrange("(o n) -> o n", o=1)
         )
         load_scale_rows(x_plane, x_scales)
-        load_run(0)
+        for r in range(3):
+            load_run(r)
         for c in range(1, CHUNKS):
-            if (c + 1) % RUN == 0 and c + 1 < CHUNKS:
-                load_run((c + 1) // RUN)
+            if c % PASSES == 0:
+                for r in range(3):
+                    load_run(3 * (c // PASSES) + r)
             load_codes(c)
 
         def spread_gain(i):
@@ -153,8 +155,7 @@ def tile_internattention_pa_kernel(
                         scalar2=None,
                         op0=ALU.mult,
                     )
-                    queue = nc.scalar if t == 0 else nc.sync
-                    queue.dma_start(out=outs[t][:, cols], in_=result[t][:, cols])
+                    nc.sync.dma_start(out=outs[t][:, cols], in_=result[t][:, cols])
             else:
                 for j in range(TILES):
                     cols = slice(NT * j, NT * (j + 1))

@@ -16,7 +16,6 @@ PASSES = HID // 512
 THIRDS = 3
 NT = 512
 TILES = HID // NT
-RUN = 2
 CHUNKS = THIRDS * PASSES
 EPS = 1e-6
 
@@ -42,8 +41,7 @@ def tile_internattention_pa_kernel(
             keep.tile([P, 2 * HID], U8, name="w_codes%d" % c, align_bytes=64) for c in range(CHUNKS)
         ]
         w_plane = [
-            keep.tile([P, RUN, HID], U8, name="w_plane%d" % r, align_bytes=64)
-            for r in range(CHUNKS // RUN)
+            keep.tile([P, PASSES, HID], U8, name="w_plane%d" % t, align_bytes=64) for t in range(THIRDS)
         ]
         warm = keep.tile([P, 2], F32, name="warm")
         ones = keep.tile([P, P], BF16, name="ones")
@@ -66,11 +64,18 @@ def tile_internattention_pa_kernel(
                     in_=rows[:, r:16:4, :].rearrange("g q n -> q g n").bitcast(I32),
                 )
 
-        def load_run(r):
-            t, a = divmod(r, PASSES // RUN)
-            load_scale_rows(
-                w_plane[r], w_qkv_scales[RUN * a : RUN * (a + 1), :, HID * t : HID * (t + 1)]
-            )
+        def load_run(t):
+            for i in range(8):
+                low = 32 * (i // 4) + i % 4
+                row = 4 * (i // 4) + i % 4
+                cuts = (0, PASSES) if i < 4 else (0, PASSES // 2, PASSES)
+                for g0, g1 in zip(cuts[:-1], cuts[1:]):
+                    nc.sync.dma_start(
+                        out=w_plane[t][low:P:64, g0:g1, :].bitcast(I32),
+                        in_=w_qkv_scales[g0:g1, row:16:8, HID * t : HID * (t + 1)]
+                        .rearrange("g q n -> q g n")
+                        .bitcast(I32),
+                    )
 
         nc.gpsimd.memset(warm[:, 0:1], 1.0)
         nc.gpsimd.memset(ones[:], 1.0)
@@ -81,22 +86,19 @@ def tile_internattention_pa_kernel(
         )
         load_codes(0)
         nc.vector.memset(x_plane[:].bitcast(I32), 0)
-        for r in range(3):
-            nc.vector.memset(w_plane[r][:].bitcast(I32), 0)
+        nc.vector.memset(w_plane[0][:].bitcast(I32), 0)
         nc.vector.memset(gain_row[:].bitcast(I32), 0)
-        for r in range(3, CHUNKS // RUN):
-            nc.vector.memset(w_plane[r][:].bitcast(I32), 0)
+        nc.vector.memset(w_plane[1][:].bitcast(I32), 0)
+        nc.vector.memset(w_plane[2][:].bitcast(I32), 0)
         nc.scalar.dma_start(out=gain_row[0:1, 0:HID], in_=q_norm_w.rearrange("(o n) -> o n", o=1))
         nc.scalar.dma_start(
             out=gain_row[0:1, HID : 2 * HID], in_=k_norm_w.rearrange("(o n) -> o n", o=1)
         )
         load_scale_rows(x_plane, x_scales)
-        for r in range(3):
-            load_run(r)
+        load_run(0)
         for c in range(1, CHUNKS):
             if c % PASSES == 0:
-                for r in range(3):
-                    load_run(3 * (c // PASSES) + r)
+                load_run(c // PASSES)
             load_codes(c)
 
         def spread_gain(i):
@@ -115,7 +117,7 @@ def tile_internattention_pa_kernel(
                         lhsT=x_codes[:, g, :].bitcast(FP4X4),
                         lhsT_scale=x_plane[:, g, :],
                         rhs=w_codes[c][:, 2 * NT * j : 2 * NT * (j + 1)].bitcast(FP4X4),
-                        rhs_scale=w_plane[c // RUN][:, c % RUN, NT * j : NT * (j + 1)],
+                        rhs_scale=w_plane[t][:, g, NT * j : NT * (j + 1)],
                         start=(g == 0),
                         stop=(g == PASSES - 1),
                     )
@@ -161,7 +163,8 @@ def tile_internattention_pa_kernel(
                     cols = slice(NT * j, NT * (j + 1))
                     if j % 2 == 0:
                         nc.vector.tensor_copy(out=result[t][:, cols], in_=acc[j][:])
-                        nc.sync.dma_start(out=outs[t][:, cols], in_=result[t][:, cols])
                     else:
                         nc.scalar.copy(out=result[t][:, cols], in_=acc[j][:])
-                        nc.scalar.dma_start(out=outs[t][:, cols], in_=result[t][:, cols])
+                    if j % 3 == 2:
+                        half = slice(NT * (j - 2), NT * (j + 1))
+                        nc.sync.dma_start(out=outs[t][:, half], in_=result[t][:, half])

@@ -85,18 +85,19 @@ def tile_internattention_pa_kernel(
             out=x_codes[:].bitcast(I32), in_=x_words.rearrange("g p b -> p g b").bitcast(I32)
         )
         load_codes(0)
+        load_codes(1)
         nc.vector.memset(x_plane[:].bitcast(I32), 0)
         nc.vector.memset(w_plane[0][:].bitcast(I32), 0)
         nc.vector.memset(gain_row[:].bitcast(I32), 0)
         nc.vector.memset(w_plane[1][:].bitcast(I32), 0)
         nc.vector.memset(w_plane[2][:].bitcast(I32), 0)
-        nc.scalar.dma_start(out=gain_row[0:1, 0:HID], in_=q_norm_w.rearrange("(o n) -> o n", o=1))
-        nc.scalar.dma_start(
-            out=gain_row[0:1, HID : 2 * HID], in_=k_norm_w.rearrange("(o n) -> o n", o=1)
-        )
         load_scale_rows(x_plane, x_scales)
         load_run(0)
-        for c in range(1, CHUNKS):
+        nc.sync.dma_start(out=gain_row[0:1, 0:HID], in_=q_norm_w.rearrange("(o n) -> o n", o=1))
+        nc.sync.dma_start(
+            out=gain_row[0:1, HID : 2 * HID], in_=k_norm_w.rearrange("(o n) -> o n", o=1)
+        )
+        for c in range(2, CHUNKS):
             if c % PASSES == 0:
                 load_run(c // PASSES)
             load_codes(c)

@@ -14,9 +14,16 @@ P = 128
 HID = 3072
 PASSES = HID // 512
 THIRDS = 3
+WIDTH = THIRDS * HID
 NT = 512
 TILES = HID // NT
 CHUNKS = THIRDS * PASSES
+PIECES = 3
+PIECE = HID // PIECES
+GROUP = 2
+GROUPS = PASSES // GROUP
+PAIRS = 8
+AHEAD = 4
 EPS = 1e-6
 
 FLOPS = 2 * P * HID * THIRDS * HID
@@ -32,16 +39,18 @@ def tile_internattention_pa_kernel(
         ctx.enter_context(tc.manual_schedule())
         keep = ctx.enter_context(tc.tile_pool(name="keep", bufs=1))
         scrap = ctx.enter_context(tc.tile_pool(name="scrap", bufs=2))
-        acc_pool = ctx.enter_context(tc.psum_pool(name="acc_pool", bufs=TILES))
-        aux_pool = ctx.enter_context(tc.psum_pool(name="aux_pool", bufs=2))
+        banks = ctx.enter_context(tc.psum_pool(name="banks", bufs=8))
 
         x_codes = keep.tile([P, PASSES, 256], U8, name="x_codes", align_bytes=64)
         x_plane = keep.tile([P, PASSES, P], U8, name="x_plane", align_bytes=64)
         w_codes = [
-            keep.tile([P, 2 * HID], U8, name="w_codes%d" % c, align_bytes=64) for c in range(CHUNKS)
+            keep.tile([P, 2 * HID], U8, name="w_codes%d" % c, align_bytes=64) for c in range(CHUNKS - 1)
+        ]
+        last_codes = [
+            keep.tile([P, 2 * PIECE], U8, name="last_codes%d" % i, align_bytes=64) for i in range(PIECES)
         ]
         w_plane = [
-            keep.tile([P, PASSES, HID], U8, name="w_plane%d" % t, align_bytes=64) for t in range(THIRDS)
+            keep.tile([P, GROUP, WIDTH], U8, name="w_plane%d" % s, align_bytes=64) for s in range(GROUPS)
         ]
         warm = keep.tile([P, 2], F32, name="warm")
         ones = keep.tile([P, P], BF16, name="ones")
@@ -57,59 +66,64 @@ def tile_internattention_pa_kernel(
                 in_=w_qkv_words[g, :, 2 * HID * t : 2 * HID * (t + 1)].bitcast(I32),
             )
 
-        def load_scale_rows(plane, rows):
-            for r in range(4):
-                nc.sync.dma_start(
-                    out=plane[r:P:32, :, :].bitcast(I32),
-                    in_=rows[:, r:16:4, :].rearrange("g q n -> q g n").bitcast(I32),
-                )
-
-        def load_run(t):
-            for i in range(8):
-                low = 32 * (i // 4) + i % 4
-                row = 4 * (i // 4) + i % 4
-                cuts = (0, PASSES) if i < 4 else (0, PASSES // 2, PASSES)
-                for g0, g1 in zip(cuts[:-1], cuts[1:]):
-                    nc.sync.dma_start(
-                        out=w_plane[t][low:P:64, g0:g1, :].bitcast(I32),
-                        in_=w_qkv_scales[g0:g1, row:16:8, HID * t : HID * (t + 1)]
-                        .rearrange("g q n -> q g n")
-                        .bitcast(I32),
-                    )
+        def load_pair(s, i, g0, g1):
+            low = 32 * (i // 4) + i % 4
+            row = 4 * (i // 4) + i % 4
+            nc.sync.dma_start(
+                out=w_plane[s][low:P:64, g0:g1, :].bitcast(I32),
+                in_=w_qkv_scales[GROUP * s + g0 : GROUP * s + g1, row:16:8, :]
+                .rearrange("g q n -> q g n")
+                .bitcast(I32),
+            )
 
         nc.gpsimd.memset(warm[:, 0:1], 1.0)
         nc.gpsimd.memset(ones[:], 1.0)
         nc.scalar.activation(out=warm[:, 1:2], in_=warm[:, 0:1], func=ACT.Sqrt)
+        nc.vector.memset(x_plane[:].bitcast(I32), 0)
+        nc.vector.memset(gain_row[:].bitcast(I32), 0)
+        for s in range(GROUPS):
+            nc.vector.memset(w_plane[s][:].bitcast(I32), 0)
 
         nc.sync.dma_start(
             out=x_codes[:].bitcast(I32), in_=x_words.rearrange("g p b -> p g b").bitcast(I32)
         )
         load_codes(0)
         load_codes(1)
-        nc.vector.memset(x_plane[:].bitcast(I32), 0)
-        nc.vector.memset(w_plane[0][:].bitcast(I32), 0)
-        nc.vector.memset(gain_row[:].bitcast(I32), 0)
-        nc.vector.memset(w_plane[1][:].bitcast(I32), 0)
-        nc.vector.memset(w_plane[2][:].bitcast(I32), 0)
-        load_scale_rows(x_plane, x_scales)
-        load_run(0)
+        for r in range(4):
+            nc.sync.dma_start(
+                out=x_plane[r:P:32, :, :].bitcast(I32),
+                in_=x_scales[:, r:16:4, :].rearrange("g q n -> q g n").bitcast(I32),
+            )
+        load_codes(2)
+        load_codes(3)
         nc.sync.dma_start(out=gain_row[0:1, 0:HID], in_=q_norm_w.rearrange("(o n) -> o n", o=1))
         nc.sync.dma_start(
             out=gain_row[0:1, HID : 2 * HID], in_=k_norm_w.rearrange("(o n) -> o n", o=1)
         )
-        for c in range(2, CHUNKS):
-            if c % PASSES == 0:
-                load_run(c // PASSES)
+        for s in range(GROUPS):
+            for i in range(PAIRS):
+                if s == GROUPS - 1 and i >= PAIRS - 2:
+                    for g0 in range(GROUP):
+                        load_pair(s, i, g0, g0 + 1)
+                else:
+                    load_pair(s, i, 0, GROUP)
+        for c in range(AHEAD, CHUNKS - 1):
             load_codes(c)
+        for i in range(PIECES):
+            first = 2 * HID * (THIRDS - 1) + 2 * PIECE * i
+            nc.sync.dma_start(
+                out=last_codes[i][:].bitcast(I32),
+                in_=w_qkv_words[PASSES - 1, :, first : first + 2 * PIECE].bitcast(I32),
+            )
 
-        def spread_gain(i):
+        for i in range(2 * TILES):
             cols = slice(NT * i, NT * (i + 1))
-            aux = aux_pool.tile([P, NT], F32, name="aux")
-            nc.tensor.matmul(out=aux[:], lhsT=ones[:], rhs=gain_row[:, cols], start=True, stop=True)
-            nc.scalar.copy(out=gain[:, cols], in_=aux[:])
+            spread = banks.tile([P, NT], F32, name="bank")
+            nc.tensor.matmul(out=spread[:], lhsT=ones[:], rhs=gain_row[:, cols], start=True, stop=True)
+            nc.scalar.copy(out=gain[:, cols], in_=spread[:])
 
         for t in range(THIRDS):
-            acc = [acc_pool.tile([P, NT], F32, name="acc") for j in range(TILES)]
+            acc = [banks.tile([P, NT], F32, name="bank") for j in range(TILES)]
             for g in range(PASSES):
                 c = PASSES * t + g
                 for j in range(TILES):
@@ -117,30 +131,39 @@ def tile_internattention_pa_kernel(
                         out=acc[j][:],
                         lhsT=x_codes[:, g, :].bitcast(FP4X4),
                         lhsT_scale=x_plane[:, g, :],
-                        rhs=w_codes[c][:, 2 * NT * j : 2 * NT * (j + 1)].bitcast(FP4X4),
-                        rhs_scale=w_plane[t][:, g, NT * j : NT * (j + 1)],
+                        rhs=(
+                            w_codes[c][:, 2 * NT * j : 2 * NT * (j + 1)]
+                            if c < CHUNKS - 1
+                            else last_codes[j // 2][:, 2 * NT * (j % 2) : 2 * NT * (j % 2 + 1)]
+                        ).bitcast(FP4X4),
+                        rhs_scale=w_plane[g // GROUP][
+                            :, g % GROUP, HID * t + NT * j : HID * t + NT * (j + 1)
+                        ],
                         start=(g == 0),
                         stop=(g == PASSES - 1),
                     )
-                if t == 0:
-                    spread_gain(2 * g)
-                    spread_gain(2 * g + 1)
-            if t < 2:
-                for j in range(TILES):
-                    cols = slice(NT * j, NT * (j + 1))
-                    squares = scrap.tile([P, NT], BF16, name="squares")
+            for j in range(TILES):
+                cols = slice(NT * j, NT * (j + 1))
+                if j % 2 == 0:
+                    nc.scalar.copy(out=result[t][:, cols], in_=acc[j][:])
+                else:
+                    nc.vector.tensor_copy(out=result[t][:, cols], in_=acc[j][:])
+                    if t == THIRDS - 1:
+                        piece = slice(NT * (j - 1), NT * (j + 1))
+                        nc.sync.dma_start(out=outs[t][:, piece], in_=result[t][:, piece])
+            if t < THIRDS - 1:
+                for h in range(2):
+                    half = slice(HID // 2 * h, HID // 2 * (h + 1))
+                    squares = scrap.tile([P, HID // 2], BF16, name="squares")
                     nc.scalar.activation(
-                        out=squares[:], in_=acc[j][:], func=ACT.Square, accum_out=stats[t][:, j : j + 1]
-                    )
-                    nc.vector.tensor_tensor(
-                        out=result[t][:, cols],
-                        in0=acc[j][:],
-                        in1=gain[:, HID * t + NT * j : HID * t + NT * (j + 1)],
-                        op=ALU.mult,
+                        out=squares[:],
+                        in_=result[t][:, half],
+                        func=ACT.Square,
+                        accum_out=stats[t][:, h : h + 1],
                     )
                 nc.vector.tensor_scalar(
-                    out=stats[t][:, 8 : 8 + TILES],
-                    in0=stats[t][:, 0:TILES],
+                    out=stats[t][:, 8:10],
+                    in0=stats[t][:, 0:2],
                     scalar1=1.0 / HID,
                     scalar2=EPS,
                     op0=ALU.mult,
@@ -150,22 +173,13 @@ def tile_internattention_pa_kernel(
                 nc.scalar.activation(out=stats[t][:, 15:16], in_=stats[t][:, 14:15], func=ACT.Sqrt)
                 nc.vector.reciprocal(out=stats[t][:, 7:8], in_=stats[t][:, 15:16])
                 for h in range(2):
-                    cols = slice(HID // 2 * h, HID // 2 * (h + 1))
-                    nc.vector.tensor_scalar(
-                        out=result[t][:, cols],
-                        in0=result[t][:, cols],
-                        scalar1=stats[t][:, 7:8],
-                        scalar2=None,
+                    half = slice(HID // 2 * h, HID // 2 * (h + 1))
+                    nc.vector.scalar_tensor_tensor(
+                        out=result[t][:, half],
+                        in0=result[t][:, half],
+                        scalar=stats[t][:, 7:8],
+                        in1=gain[:, HID * t + HID // 2 * h : HID * t + HID // 2 * (h + 1)],
                         op0=ALU.mult,
+                        op1=ALU.mult,
                     )
-                    nc.sync.dma_start(out=outs[t][:, cols], in_=result[t][:, cols])
-            else:
-                for j in range(TILES):
-                    cols = slice(NT * j, NT * (j + 1))
-                    if j % 2 == 0:
-                        nc.vector.tensor_copy(out=result[t][:, cols], in_=acc[j][:])
-                    else:
-                        nc.scalar.copy(out=result[t][:, cols], in_=acc[j][:])
-                    if j % 3 == 2:
-                        half = slice(NT * (j - 2), NT * (j + 1))
-                        nc.sync.dma_start(out=outs[t][:, half], in_=result[t][:, half])
+                    nc.sync.dma_start(out=outs[t][:, half], in_=result[t][:, half])

@@ -41,22 +41,22 @@ def tile_internattention_pa_kernel(
         scrap = ctx.enter_context(tc.tile_pool(name="scrap", bufs=2))
         banks = ctx.enter_context(tc.psum_pool(name="banks", bufs=8))
 
-        x_codes = keep.tile([P, PASSES, 256], U8, name="x_codes", align_bytes=64)
-        x_plane = keep.tile([P, PASSES, P], U8, name="x_plane", align_bytes=64)
+        x_codes = keep.tile([P, PASSES, 256], U8, name="x_codes", align_bytes=256)
+        x_plane = keep.tile([P, PASSES, P], U8, name="x_plane", align_bytes=256)
         w_codes = [
-            keep.tile([P, 2 * HID], U8, name="w_codes%d" % c, align_bytes=64) for c in range(CHUNKS - 1)
+            keep.tile([P, 2 * HID], U8, name="w_codes%d" % c, align_bytes=256) for c in range(CHUNKS - 1)
         ]
         last_codes = [
-            keep.tile([P, 2 * PIECE], U8, name="last_codes%d" % i, align_bytes=64) for i in range(PIECES)
+            keep.tile([P, 2 * PIECE], U8, name="last_codes%d" % i, align_bytes=256) for i in range(PIECES)
         ]
         w_plane = [
-            keep.tile([P, GROUP, WIDTH], U8, name="w_plane%d" % s, align_bytes=64) for s in range(GROUPS)
+            keep.tile([P, GROUP, WIDTH], U8, name="w_plane%d" % s, align_bytes=256) for s in range(GROUPS)
         ]
         warm = keep.tile([P, 2], F32, name="warm")
         ones = keep.tile([P, P], BF16, name="ones")
-        gain_row = keep.tile([P, 2 * HID], BF16, name="gain_row")
+        gain_row = keep.tile([P, 2 * HID], BF16, name="gain_row", align_bytes=256)
         gain = keep.tile([P, 2 * HID], BF16, name="gain")
-        result = [keep.tile([P, HID], F32, name="result%d" % t) for t in range(THIRDS)]
+        result = [keep.tile([P, HID], F32, name="result%d" % t, align_bytes=256) for t in range(THIRDS)]
         stats = [keep.tile([P, 16], F32, name="stats%d" % t) for t in range(2)]
 
         def load_codes(c):
@@ -182,4 +182,4 @@ def tile_internattention_pa_kernel(
                         op0=ALU.mult,
                         op1=ALU.mult,
                     )
-                    nc.sync.dma_start(out=outs[t][:, half], in_=result[t][:, half])
+                nc.sync.dma_start(out=outs[t][:, :], in_=result[t][:])

@@ -12,19 +12,39 @@ ALU = mybir.AluOpType
 
 P = 128
 HID = 3072
-PASSES = HID // 512
+PASS_K = 512
+PASSES = HID // PASS_K
 THIRDS = 3
+NORMED = 2
 WIDTH = THIRDS * HID
 NT = 512
 TILES = HID // NT
+BANKS = 8
+CODE_BYTES = 2
 CHUNKS = THIRDS * PASSES
-PIECES = 3
+PIECES = 1
 PIECE = HID // PIECES
+PIECE_TILES = PIECE // NT
 GROUP = 2
 GROUPS = PASSES // GROUP
-PAIRS = 8
+ROWS = 16
+QUADRANT = 32
+QUAD_ROWS = ROWS * QUADRANT // P
+PAIRS = ROWS // 2
+SPLIT_PAIRS = 2
 AHEAD = 4
+X_AHEAD = 2
+ALIGN = 256
+HALVES = 2
+HALF = HID // HALVES
 EPS = 1e-6
+
+SUMS = 0
+SCALED = 8
+MEAN = 14
+RMS = 15
+INV = 7
+STATS = 16
 
 FLOPS = 2 * P * HID * THIRDS * HID
 
@@ -38,41 +58,43 @@ def tile_internattention_pa_kernel(
     with ExitStack() as ctx:
         ctx.enter_context(tc.manual_schedule())
         keep = ctx.enter_context(tc.tile_pool(name="keep", bufs=1))
-        scrap = ctx.enter_context(tc.tile_pool(name="scrap", bufs=2))
-        banks = ctx.enter_context(tc.psum_pool(name="banks", bufs=8))
+        scrap = ctx.enter_context(tc.tile_pool(name="scrap", bufs=HALVES))
+        banks = ctx.enter_context(tc.psum_pool(name="banks", bufs=BANKS))
 
-        x_codes = keep.tile([P, PASSES, 256], U8, name="x_codes", align_bytes=256)
-        x_plane = keep.tile([P, PASSES, P], U8, name="x_plane", align_bytes=256)
+        x_codes = keep.tile([P, PASSES, CODE_BYTES * P], U8, name="x_codes", align_bytes=ALIGN)
+        x_plane = keep.tile([P, PASSES, P], U8, name="x_plane", align_bytes=ALIGN)
         w_codes = [
-            keep.tile([P, 2 * HID], U8, name="w_codes%d" % c, align_bytes=256) for c in range(CHUNKS - 1)
+            keep.tile([P, CODE_BYTES * HID], U8, name="w_codes%d" % chunk, align_bytes=ALIGN)
+            for chunk in range(CHUNKS - 1)
         ]
         last_codes = [
-            keep.tile([P, 2 * PIECE], U8, name="last_codes%d" % i, align_bytes=256) for i in range(PIECES)
+            keep.tile([P, CODE_BYTES * PIECE], U8, name="last_codes%d" % piece, align_bytes=ALIGN)
+            for piece in range(PIECES)
         ]
         w_plane = [
-            keep.tile([P, GROUP, WIDTH], U8, name="w_plane%d" % s, align_bytes=256) for s in range(GROUPS)
+            keep.tile([P, GROUP, WIDTH], U8, name="w_plane%d" % group, align_bytes=ALIGN) for group in range(GROUPS)
         ]
         warm = keep.tile([P, 2], F32, name="warm")
         ones = keep.tile([P, P], BF16, name="ones")
-        gain_row = keep.tile([P, 2 * HID], BF16, name="gain_row", align_bytes=256)
-        gain = keep.tile([P, 2 * HID], BF16, name="gain")
-        result = [keep.tile([P, HID], F32, name="result%d" % t, align_bytes=256) for t in range(THIRDS)]
-        stats = [keep.tile([P, 16], F32, name="stats%d" % t) for t in range(2)]
+        gain_row = keep.tile([P, NORMED * HID], BF16, name="gain_row", align_bytes=ALIGN)
+        gain = keep.tile([P, NORMED * HID], BF16, name="gain")
+        result = [keep.tile([P, HID], F32, name="result%d" % third, align_bytes=ALIGN) for third in range(THIRDS)]
+        stats = [keep.tile([P, STATS], F32, name="stats%d" % third) for third in range(NORMED)]
 
-        def load_codes(c):
-            t, g = divmod(c, PASSES)
+        def load_codes(chunk):
+            third, g = divmod(chunk, PASSES)
             nc.sync.dma_start(
-                out=w_codes[c][:].bitcast(I32),
-                in_=w_qkv_words[g, :, 2 * HID * t : 2 * HID * (t + 1)].bitcast(I32),
+                out=w_codes[chunk][:].bitcast(I32),
+                in_=w_qkv_words[g, :, CODE_BYTES * HID * third : CODE_BYTES * HID * (third + 1)].bitcast(I32),
             )
 
-        def load_pair(s, i, g0, g1):
-            low = 32 * (i // 4) + i % 4
-            row = 4 * (i // 4) + i % 4
+        def load_pair(group, pair, first, stop):
+            low = QUADRANT * (pair // QUAD_ROWS) + pair % QUAD_ROWS
+            row = QUAD_ROWS * (pair // QUAD_ROWS) + pair % QUAD_ROWS
             nc.sync.dma_start(
-                out=w_plane[s][low:P:64, g0:g1, :].bitcast(I32),
-                in_=w_qkv_scales[GROUP * s + g0 : GROUP * s + g1, row:16:8, :]
-                .rearrange("g q n -> q g n")
+                out=w_plane[group][low : P : 2 * QUADRANT, first:stop, :].bitcast(I32),
+                in_=w_qkv_scales[GROUP * group + first : GROUP * group + stop, row:ROWS:PAIRS, :]
+                .rearrange("g u n -> u g n")
                 .bitcast(I32),
             )
 
@@ -81,105 +103,105 @@ def tile_internattention_pa_kernel(
         nc.scalar.activation(out=warm[:, 1:2], in_=warm[:, 0:1], func=ACT.Sqrt)
         nc.vector.memset(x_plane[:].bitcast(I32), 0)
         nc.vector.memset(gain_row[:].bitcast(I32), 0)
-        for s in range(GROUPS):
-            nc.vector.memset(w_plane[s][:].bitcast(I32), 0)
+        for group in range(GROUPS):
+            nc.vector.memset(w_plane[group][:].bitcast(I32), 0)
 
-        nc.sync.dma_start(
-            out=x_codes[:].bitcast(I32), in_=x_words.rearrange("g p b -> p g b").bitcast(I32)
-        )
-        load_codes(0)
-        load_codes(1)
-        for r in range(4):
+        nc.sync.dma_start(out=x_codes[:].bitcast(I32), in_=x_words.rearrange("g p b -> p g b").bitcast(I32))
+        for chunk in range(X_AHEAD):
+            load_codes(chunk)
+        for r in range(QUAD_ROWS):
             nc.sync.dma_start(
-                out=x_plane[r:P:32, :, :].bitcast(I32),
-                in_=x_scales[:, r:16:4, :].rearrange("g q n -> q g n").bitcast(I32),
+                out=x_plane[r:P:QUADRANT, :, :].bitcast(I32),
+                in_=x_scales[:, r:ROWS:QUAD_ROWS, :].rearrange("g u n -> u g n").bitcast(I32),
             )
-        load_codes(2)
-        load_codes(3)
+        for chunk in range(X_AHEAD, AHEAD):
+            load_codes(chunk)
         nc.sync.dma_start(out=gain_row[0:1, 0:HID], in_=q_norm_w.rearrange("(o n) -> o n", o=1))
-        nc.sync.dma_start(
-            out=gain_row[0:1, HID : 2 * HID], in_=k_norm_w.rearrange("(o n) -> o n", o=1)
-        )
-        for s in range(GROUPS):
-            for i in range(PAIRS):
-                if s == GROUPS - 1 and i >= PAIRS - 2:
-                    for g0 in range(GROUP):
-                        load_pair(s, i, g0, g0 + 1)
+        nc.sync.dma_start(out=gain_row[0:1, HID : NORMED * HID], in_=k_norm_w.rearrange("(o n) -> o n", o=1))
+        for group in range(GROUPS):
+            for pair in range(PAIRS):
+                if group == GROUPS - 1 and pair >= PAIRS - SPLIT_PAIRS:
+                    for g_in_group in range(GROUP):
+                        load_pair(group, pair, g_in_group, g_in_group + 1)
                 else:
-                    load_pair(s, i, 0, GROUP)
-        for c in range(AHEAD, CHUNKS - 1):
-            load_codes(c)
-        for i in range(PIECES):
-            first = 2 * HID * (THIRDS - 1) + 2 * PIECE * i
+                    load_pair(group, pair, 0, GROUP)
+        for chunk in range(AHEAD, CHUNKS - 1):
+            load_codes(chunk)
+        for piece in range(PIECES):
+            first_byte = CODE_BYTES * (HID * (THIRDS - 1) + PIECE * piece)
             nc.sync.dma_start(
-                out=last_codes[i][:].bitcast(I32),
-                in_=w_qkv_words[PASSES - 1, :, first : first + 2 * PIECE].bitcast(I32),
+                out=last_codes[piece][:].bitcast(I32),
+                in_=w_qkv_words[PASSES - 1, :, first_byte : first_byte + CODE_BYTES * PIECE].bitcast(I32),
             )
 
-        for i in range(2 * TILES):
-            cols = slice(NT * i, NT * (i + 1))
+        for col_tile in range(NORMED * TILES):
+            cols = slice(NT * col_tile, NT * (col_tile + 1))
             spread = banks.tile([P, NT], F32, name="bank")
             nc.tensor.matmul(out=spread[:], lhsT=ones[:], rhs=gain_row[:, cols], start=True, stop=True)
             nc.scalar.copy(out=gain[:, cols], in_=spread[:])
 
-        for t in range(THIRDS):
-            acc = [banks.tile([P, NT], F32, name="bank") for j in range(TILES)]
+        for third in range(THIRDS):
+            acc = [banks.tile([P, NT], F32, name="bank") for col_tile in range(TILES)]
             for g in range(PASSES):
-                c = PASSES * t + g
-                for j in range(TILES):
+                chunk = PASSES * third + g
+                for col_tile in range(TILES):
+                    in_piece = col_tile % PIECE_TILES
                     nc.tensor.matmul_mx(
-                        out=acc[j][:],
+                        out=acc[col_tile][:],
                         lhsT=x_codes[:, g, :].bitcast(FP4X4),
                         lhsT_scale=x_plane[:, g, :],
                         rhs=(
-                            w_codes[c][:, 2 * NT * j : 2 * NT * (j + 1)]
-                            if c < CHUNKS - 1
-                            else last_codes[j // 2][:, 2 * NT * (j % 2) : 2 * NT * (j % 2 + 1)]
+                            w_codes[chunk][:, CODE_BYTES * NT * col_tile : CODE_BYTES * NT * (col_tile + 1)]
+                            if chunk < CHUNKS - 1
+                            else last_codes[col_tile // PIECE_TILES][
+                                :, CODE_BYTES * NT * in_piece : CODE_BYTES * NT * (in_piece + 1)
+                            ]
                         ).bitcast(FP4X4),
                         rhs_scale=w_plane[g // GROUP][
-                            :, g % GROUP, HID * t + NT * j : HID * t + NT * (j + 1)
+                            :, g % GROUP, HID * third + NT * col_tile : HID * third + NT * (col_tile + 1)
                         ],
                         start=(g == 0),
                         stop=(g == PASSES - 1),
                     )
-            for j in range(TILES):
-                cols = slice(NT * j, NT * (j + 1))
-                if j % 2 == 0:
-                    nc.scalar.copy(out=result[t][:, cols], in_=acc[j][:])
+            for col_tile in range(TILES):
+                cols = slice(NT * col_tile, NT * (col_tile + 1))
+                if col_tile % 2 == 0:
+                    nc.scalar.copy(out=result[third][:, cols], in_=acc[col_tile][:])
                 else:
-                    nc.vector.tensor_copy(out=result[t][:, cols], in_=acc[j][:])
-                    if t == THIRDS - 1:
-                        piece = slice(NT * (j - 1), NT * (j + 1))
-                        nc.sync.dma_start(out=outs[t][:, piece], in_=result[t][:, piece])
-            if t < THIRDS - 1:
-                for h in range(2):
-                    half = slice(HID // 2 * h, HID // 2 * (h + 1))
-                    squares = scrap.tile([P, HID // 2], BF16, name="squares")
+                    nc.vector.tensor_copy(out=result[third][:, cols], in_=acc[col_tile][:])
+                if third >= NORMED and (col_tile + 1) % PIECE_TILES == 0:
+                    done = slice(NT * (col_tile + 1) - PIECE, NT * (col_tile + 1))
+                    nc.sync.dma_start(out=outs[third][:, done], in_=result[third][:, done])
+            if third < NORMED:
+                for h in range(HALVES):
+                    squares = scrap.tile([P, HALF], BF16, name="squares")
                     nc.scalar.activation(
                         out=squares[:],
-                        in_=result[t][:, half],
+                        in_=result[third][:, HALF * h : HALF * (h + 1)],
                         func=ACT.Square,
-                        accum_out=stats[t][:, h : h + 1],
+                        accum_out=stats[third][:, SUMS + h : SUMS + h + 1],
                     )
                 nc.vector.tensor_scalar(
-                    out=stats[t][:, 8:10],
-                    in0=stats[t][:, 0:2],
+                    out=stats[third][:, SCALED : SCALED + HALVES],
+                    in0=stats[third][:, SUMS : SUMS + HALVES],
                     scalar1=1.0 / HID,
                     scalar2=EPS,
                     op0=ALU.mult,
                     op1=ALU.add,
-                    accum_out=stats[t][:, 14:15],
+                    accum_out=stats[third][:, MEAN : MEAN + 1],
                 )
-                nc.scalar.activation(out=stats[t][:, 15:16], in_=stats[t][:, 14:15], func=ACT.Sqrt)
-                nc.vector.reciprocal(out=stats[t][:, 7:8], in_=stats[t][:, 15:16])
-                for h in range(2):
-                    half = slice(HID // 2 * h, HID // 2 * (h + 1))
+                nc.scalar.activation(
+                    out=stats[third][:, RMS : RMS + 1], in_=stats[third][:, MEAN : MEAN + 1], func=ACT.Sqrt
+                )
+                nc.vector.reciprocal(out=stats[third][:, INV : INV + 1], in_=stats[third][:, RMS : RMS + 1])
+                for h in range(HALVES):
+                    half = slice(HALF * h, HALF * (h + 1))
                     nc.vector.scalar_tensor_tensor(
-                        out=result[t][:, half],
-                        in0=result[t][:, half],
-                        scalar=stats[t][:, 7:8],
-                        in1=gain[:, HID * t + HID // 2 * h : HID * t + HID // 2 * (h + 1)],
+                        out=result[third][:, half],
+                        in0=result[third][:, half],
+                        scalar=stats[third][:, INV : INV + 1],
+                        in1=gain[:, HID * third + HALF * h : HID * third + HALF * (h + 1)],
                         op0=ALU.mult,
                         op1=ALU.mult,
                     )
-                nc.sync.dma_start(out=outs[t][:, :], in_=result[t][:])
+                nc.sync.dma_start(out=outs[third][:, :], in_=result[third][:])

@@ -31,7 +31,7 @@ ROWS = 16
 QUADRANT = 32
 QUAD_ROWS = ROWS * QUADRANT // P
 PAIRS = ROWS // 2
-SPLIT_PAIRS = 2
+SPLIT_PAIRS = 4
 AHEAD = 4
 X_AHEAD = 2
 ALIGN = 256

from contextlib import ExitStack

import concourse.mybir as mybir

F32 = mybir.dt.float32
BF16 = mybir.dt.bfloat16
I32 = mybir.dt.int32
U8 = mybir.dt.uint8
FP4X4 = mybir.dt.float4_e2m1fn_x4
ACT = mybir.ActivationFunctionType
ALU = mybir.AluOpType

P = 128
HID = 3072
PASS_K = 512
PASSES = HID // PASS_K
THIRDS = 3
NORMED = 2
WIDTH = THIRDS * HID
NT = 512
TILES = HID // NT
BANKS = 8
CODE_BYTES = 2
CHUNKS = THIRDS * PASSES
PIECES = 1
PIECE = HID // PIECES
PIECE_TILES = PIECE // NT
GROUP = 2
GROUPS = PASSES // GROUP
ROWS = 16
QUADRANT = 32
QUAD_ROWS = ROWS * QUADRANT // P
PAIRS = ROWS // 2
SPLIT_PAIRS = 4
AHEAD = 4
X_AHEAD = 2
ALIGN = 256
HALVES = 2
HALF = HID // HALVES
EPS = 1e-6

SUMS = 0
SCALED = 8
MEAN = 14
RMS = 15
INV = 7
STATS = 16

FLOPS = 2 * P * HID * THIRDS * HID


def tile_internattention_pa_kernel(
    tc, x_words, x_scales, w_qkv_words, w_qkv_scales, q_norm_w, k_norm_w, out_0, out_1, out_2
):
    nc = tc.nc
    outs = [out_0.flatten_outer_dims(), out_1.flatten_outer_dims(), out_2.flatten_outer_dims()]

    with ExitStack() as ctx:
        ctx.enter_context(tc.manual_schedule())
        keep = ctx.enter_context(tc.tile_pool(name="keep", bufs=1))
        scrap = ctx.enter_context(tc.tile_pool(name="scrap", bufs=HALVES))
        banks = ctx.enter_context(tc.psum_pool(name="banks", bufs=BANKS))

        x_codes = keep.tile([P, PASSES, CODE_BYTES * P], U8, name="x_codes", align_bytes=ALIGN)
        x_plane = keep.tile([P, PASSES, P], U8, name="x_plane", align_bytes=ALIGN)
        w_codes = [
            keep.tile([P, CODE_BYTES * HID], U8, name="w_codes%d" % chunk, align_bytes=ALIGN)
            for chunk in range(CHUNKS - 1)
        ]
        last_codes = [
            keep.tile([P, CODE_BYTES * PIECE], U8, name="last_codes%d" % piece, align_bytes=ALIGN)
            for piece in range(PIECES)
        ]
        w_plane = [
            keep.tile([P, GROUP, WIDTH], U8, name="w_plane%d" % group, align_bytes=ALIGN) for group in range(GROUPS)
        ]
        warm = keep.tile([P, 2], F32, name="warm")
        ones = keep.tile([P, P], BF16, name="ones")
        gain_row = keep.tile([P, NORMED * HID], BF16, name="gain_row", align_bytes=ALIGN)
        gain = keep.tile([P, NORMED * HID], BF16, name="gain")
        result = [keep.tile([P, HID], F32, name="result%d" % third, align_bytes=ALIGN) for third in range(THIRDS)]
        stats = [keep.tile([P, STATS], F32, name="stats%d" % third) for third in range(NORMED)]

        def load_codes(chunk):
            third, g = divmod(chunk, PASSES)
            nc.sync.dma_start(
                out=w_codes[chunk][:].bitcast(I32),
                in_=w_qkv_words[g, :, CODE_BYTES * HID * third : CODE_BYTES * HID * (third + 1)].bitcast(I32),
            )

        def load_pair(group, pair, first, stop):
            low = QUADRANT * (pair // QUAD_ROWS) + pair % QUAD_ROWS
            row = QUAD_ROWS * (pair // QUAD_ROWS) + pair % QUAD_ROWS
            nc.sync.dma_start(
                out=w_plane[group][low : P : 2 * QUADRANT, first:stop, :].bitcast(I32),
                in_=w_qkv_scales[GROUP * group + first : GROUP * group + stop, row:ROWS:PAIRS, :]
                .rearrange("g u n -> u g n")
                .bitcast(I32),
            )

        nc.gpsimd.memset(warm[:, 0:1], 1.0)
        nc.gpsimd.memset(ones[:], 1.0)
        nc.scalar.activation(out=warm[:, 1:2], in_=warm[:, 0:1], func=ACT.Sqrt)
        nc.vector.memset(x_plane[:].bitcast(I32), 0)
        nc.vector.memset(gain_row[:].bitcast(I32), 0)
        for group in range(GROUPS):
            nc.vector.memset(w_plane[group][:].bitcast(I32), 0)

        nc.sync.dma_start(out=x_codes[:].bitcast(I32), in_=x_words.rearrange("g p b -> p g b").bitcast(I32))
        for chunk in range(X_AHEAD):
            load_codes(chunk)
        for r in range(QUAD_ROWS):
            nc.sync.dma_start(
                out=x_plane[r:P:QUADRANT, :, :].bitcast(I32),
                in_=x_scales[:, r:ROWS:QUAD_ROWS, :].rearrange("g u n -> u g n").bitcast(I32),
            )
        for chunk in range(X_AHEAD, AHEAD):
            load_codes(chunk)
        nc.sync.dma_start(out=gain_row[0:1, 0:HID], in_=q_norm_w.rearrange("(o n) -> o n", o=1))
        nc.sync.dma_start(out=gain_row[0:1, HID : NORMED * HID], in_=k_norm_w.rearrange("(o n) -> o n", o=1))
        for group in range(GROUPS):
            for pair in range(PAIRS):
                if group == GROUPS - 1 and pair >= PAIRS - SPLIT_PAIRS:
                    for g_in_group in range(GROUP):
                        load_pair(group, pair, g_in_group, g_in_group + 1)
                else:
                    load_pair(group, pair, 0, GROUP)
        for chunk in range(AHEAD, CHUNKS - 1):
            load_codes(chunk)
        for piece in range(PIECES):
            first_byte = CODE_BYTES * (HID * (THIRDS - 1) + PIECE * piece)
            nc.sync.dma_start(
                out=last_codes[piece][:].bitcast(I32),
                in_=w_qkv_words[PASSES - 1, :, first_byte : first_byte + CODE_BYTES * PIECE].bitcast(I32),
            )

        for col_tile in range(NORMED * TILES):
            cols = slice(NT * col_tile, NT * (col_tile + 1))
            spread = banks.tile([P, NT], F32, name="bank")
            nc.tensor.matmul(out=spread[:], lhsT=ones[:], rhs=gain_row[:, cols], start=True, stop=True)
            nc.scalar.copy(out=gain[:, cols], in_=spread[:])

        for third in range(THIRDS):
            acc = [banks.tile([P, NT], F32, name="bank") for col_tile in range(TILES)]
            for g in range(PASSES):
                chunk = PASSES * third + g
                for col_tile in range(TILES):
                    in_piece = col_tile % PIECE_TILES
                    nc.tensor.matmul_mx(
                        out=acc[col_tile][:],
                        lhsT=x_codes[:, g, :].bitcast(FP4X4),
                        lhsT_scale=x_plane[:, g, :],
                        rhs=(
                            w_codes[chunk][:, CODE_BYTES * NT * col_tile : CODE_BYTES * NT * (col_tile + 1)]
                            if chunk < CHUNKS - 1
                            else last_codes[col_tile // PIECE_TILES][
                                :, CODE_BYTES * NT * in_piece : CODE_BYTES * NT * (in_piece + 1)
                            ]
                        ).bitcast(FP4X4),
                        rhs_scale=w_plane[g // GROUP][
                            :, g % GROUP, HID * third + NT * col_tile : HID * third + NT * (col_tile + 1)
                        ],
                        start=(g == 0),
                        stop=(g == PASSES - 1),
                    )
            for col_tile in range(TILES):
                cols = slice(NT * col_tile, NT * (col_tile + 1))
                if col_tile % 2 == 0:
                    nc.scalar.copy(out=result[third][:, cols], in_=acc[col_tile][:])
                else:
                    nc.vector.tensor_copy(out=result[third][:, cols], in_=acc[col_tile][:])
                if third >= NORMED and (col_tile + 1) % PIECE_TILES == 0:
                    done = slice(NT * (col_tile + 1) - PIECE, NT * (col_tile + 1))
                    nc.sync.dma_start(out=outs[third][:, done], in_=result[third][:, done])
            if third < NORMED:
                for h in range(HALVES):
                    squares = scrap.tile([P, HALF], BF16, name="squares")
                    nc.scalar.activation(
                        out=squares[:],
                        in_=result[third][:, HALF * h : HALF * (h + 1)],
                        func=ACT.Square,
                        accum_out=stats[third][:, SUMS + h : SUMS + h + 1],
                    )
                nc.vector.tensor_scalar(
                    out=stats[third][:, SCALED : SCALED + HALVES],
                    in0=stats[third][:, SUMS : SUMS + HALVES],
                    scalar1=1.0 / HID,
                    scalar2=EPS,
                    op0=ALU.mult,
                    op1=ALU.add,
                    accum_out=stats[third][:, MEAN : MEAN + 1],
                )
                nc.scalar.activation(
                    out=stats[third][:, RMS : RMS + 1], in_=stats[third][:, MEAN : MEAN + 1], func=ACT.Sqrt
                )
                nc.vector.reciprocal(out=stats[third][:, INV : INV + 1], in_=stats[third][:, RMS : RMS + 1])
                for h in range(HALVES):
                    half = slice(HALF * h, HALF * (h + 1))
                    nc.vector.scalar_tensor_tensor(
                        out=result[third][:, half],
                        in0=result[third][:, half],
                        scalar=stats[third][:, INV : INV + 1],
                        in1=gain[:, HID * third + HALF * h : HID * third + HALF * (h + 1)],
                        op0=ALU.mult,
                        op1=ALU.mult,
                    )
                nc.sync.dma_start(out=outs[third][:, :], in_=result[third][:])
